import numpy as np
import ml_dtypes


def mxq(x, axis, fmt="e4m3"):
    dtype, down = {"e4m3": (ml_dtypes.float8_e4m3fn, 7), "e5m2": (ml_dtypes.float8_e5m2, 14)}[fmt]
    v = np.moveaxis(np.asarray(x, np.float32).astype(ml_dtypes.bfloat16).astype(np.float64), axis, -1)
    blocks = v.reshape(v.shape[:-1] + (-1, 32))
    amax = np.abs(blocks).max(-1, keepdims=True)
    byte = np.maximum(np.where(amax > 0, np.frexp(amax)[1] - 1 + 127, 0) - down, 1)
    scale = np.exp2(byte - 127.0)
    codes = (blocks / scale).astype(np.float32).astype(dtype).astype(np.float64)
    return np.moveaxis((codes * scale).reshape(v.shape), -1, axis)


WIDE = False


def mx_kscale(k):
    if not WIDE:
        return np.ones(k)
    levels = np.array([10, -10, 5, -5, 0])
    if k % 512:
        return np.exp2(np.random.permutation(np.resize(levels, k // 32))).repeat(32)
    a = np.empty((k // 512, 16))
    for p in range(k // 512):
        a[p, :8] = np.random.permutation(np.resize(levels, 8))
        for g in range(8):
            far = levels[np.abs(levels - a[p, g]) >= 10]
            a[p, g + 8] = far[np.random.randint(len(far))]
    return np.exp2(a.ravel()).repeat(32)


BF16 = ml_dtypes.bfloat16


def bf(x):
    return np.asarray(x, np.float32).astype(BF16)


def f64(x):
    return np.asarray(x).astype(np.float64)


B, S, D, M, R = 128, 4, 512, 8, 512
LN_EPS = 1e-5


def sigmoid(v):
    return 1.0 / (1.0 + np.exp(-v))


def layer_norm(x):
    mu = np.mean(x, axis=-1, keepdims=True)
    var = np.var(x, axis=-1, keepdims=True)
    return (x - mu) / np.sqrt(var + LN_EPS)


def setup_inputs():
    s, t = mx_kscale(D), mx_kscale(R)
    return {"interface": bf(np.random.standard_normal((B, S, D)) * np.sqrt(S) * s),
            "memory": bf(0.5 + np.random.standard_normal((B, M, D))),
            "W_write_key": bf(np.random.standard_normal((R, D)) / np.sqrt(D) / s[None, :] * t[:, None]),
            "W_write_erase": bf(np.random.standard_normal((D, R)) * 1.5 / np.sqrt(R) / t[None, :]),
            "W_write_add": bf(np.random.standard_normal((D, R)) / np.sqrt(R) / t[None, :])}


def reference(interface, memory, W_write_key, W_write_erase, W_write_add):
    i_mean = np.mean(f64(interface), axis=1)
    i_proj = mxq(i_mean, 1, "e4m3") @ mxq(f64(W_write_key), 1, "e4m3").T
    pq = mxq(i_proj, 1, "e4m3")
    erase = sigmoid(pq @ mxq(f64(W_write_erase), 1, "e4m3").T)[:, None, :]
    add = (pq @ mxq(f64(W_write_add), 1, "e4m3").T)[:, None, :]
    return layer_norm(f64(memory) * (1.0 - erase) + add)

@@ -1,0 +1,242 @@
+from contextlib import ExitStack
+
+import concourse.mybir as mybir
+from concourse.masks import make_identity
+
+F32 = mybir.dt.float32
+BF16 = mybir.dt.bfloat16
+U32 = mybir.dt.uint32
+U8 = mybir.dt.uint8
+FP8X4 = mybir.dt.float8_e4m3fn_x4
+ALU = mybir.AluOpType
+ACT = mybir.ActivationFunctionType
+
+P = 128
+POSITIONS = 4
+SLOTS = 8
+D = 512
+PACK = 4
+CHUNKS = D // P
+WORDS = D // 2
+LN_EPS = 1e-5
+VECTOR_NORM_SLOTS = 4
+GPSIMD_COLUMNS = 256
+VECTOR_COLUMNS = D - GPSIMD_COLUMNS
+LAG = 2
+
+FLOPS = 3 * 2 * P * D * D
+
+
+def transpose_words(nc, banks, pool, weight_sb, identity, copy_out, name):
+    words = weight_sb[:].bitcast(F32)
+    grouped = pool.tile([P, D * PACK], BF16, align_bytes=64, name=name + "_grouped")
+    grouped_words = grouped[:].bitcast(F32)
+    for half in range(2):
+        bank = banks.tile([P, 2, 2 * P], F32, tag="bank", name=name + "_bank")
+        for u in range(2):
+            for j in range(2):
+                c = 2 * half + j
+                nc.tensor.transpose(
+                    bank[:, u, P * j : P * (j + 1)], words[:, WORDS * c + u : WORDS * (c + 1) : 2], identity[:]
+                )
+        copy_out(
+            out=grouped_words[:, D * half : D * (half + 1)].rearrange("p (n u) -> p n u", u=2),
+            in_=bank[:].rearrange("p u n -> p n u"),
+        )
+    return grouped
+
+
+def quantise(nc, pool, grouped, columns, name):
+    codes = pool.tile([P, columns], U32, align_bytes=64, name=name + "_codes")
+    scales = pool.tile([P, columns], U8, align_bytes=64, name=name + "_scales")
+    nc.vector.quantize_mx(out=codes[:].bitcast(FP8X4), scales=scales[:], in_=grouped[:])
+    return codes, scales
+
+
+def one_pass(nc, acc, stationary, moving):
+    nc.tensor.matmul_mx(
+        out=acc,
+        lhsT=stationary[0].bitcast(FP8X4),
+        lhsT_scale=stationary[1],
+        rhs=moving[0].bitcast(FP8X4),
+        rhs_scale=moving[1],
+        start=True,
+        stop=True,
+    )
+
+
+def tile_ultralightweightmemory_pa_s_kernel(
+    tc, interface, memory, W_write_key, W_write_erase, W_write_add, out
+):
+    nc = tc.nc
+    with ExitStack() as stack:
+        pool = stack.enter_context(tc.tile_pool(name="resident", bufs=1))
+        banks = stack.enter_context(tc.psum_pool(name="banks", bufs=4))
+        sums = stack.enter_context(tc.psum_pool(name="sums", bufs=1))
+        stack.enter_context(tc.manual_schedule())
+
+        iface_sb = pool.tile([P, POSITIONS, D], BF16)
+        nc.sync.dma_start(out=iface_sb[:], in_=interface)
+        key_sb = pool.tile([P, CHUNKS * D], BF16)
+        key_rows = W_write_key.rearrange("(q c) k -> q (c k)", c=CHUNKS)
+        for u in range(2):
+            half = slice(2 * D * u, 2 * D * (u + 1))
+            nc.sync.dma_start(out=key_sb[:, half], in_=key_rows[:, half])
+        erase_sb = pool.tile([P, CHUNKS * D], BF16)
+        nc.sync.dma_start(
+            out=erase_sb[:].rearrange("q (c k) -> q c k", c=CHUNKS),
+            in_=W_write_erase.rearrange("(c q) k -> q c k", q=P),
+        )
+        add_sb = pool.tile([P, CHUNKS * D], BF16)
+        nc.sync.dma_start(
+            out=add_sb[:].rearrange("q (c k) -> q c k", c=CHUNKS),
+            in_=W_write_add.rearrange("(c q) k -> q c k", q=P),
+        )
+        memory_sb = pool.tile([P, SLOTS, D], BF16)
+        nc.sync.dma_start(out=memory_sb[:], in_=memory)
+
+        identity = pool.tile([P, P], F32)
+        make_identity(nc, identity[:])
+        eps_col = pool.tile([P, 1], F32)
+        nc.vector.memset(eps_col[:], LN_EPS)
+        warm_col = pool.tile([P, 2], F32)
+        nc.scalar.activation(out=warm_col[:, 0:1], in_=eps_col[:], func=ACT.Sigmoid)
+
+        pair_sums = pool.tile([P, 2, D], F32)
+        nc.vector.tensor_tensor(out=pair_sums[:], in0=iface_sb[:, 0:2, :], in1=iface_sb[:, 2:4, :], op=ALU.add)
+        position_sum = pool.tile([P, D], F32)
+        nc.vector.tensor_tensor(
+            out=position_sum[:].rearrange("b (t q) -> b t q", t=PACK),
+            in0=pair_sums[:, 0, :].rearrange("b (q t) -> b t q", t=PACK),
+            in1=pair_sums[:, 1, :].rearrange("b (q t) -> b t q", t=PACK),
+            op=ALU.add,
+        )
+
+        key_grouped = transpose_words(nc, banks, pool, key_sb, identity, nc.scalar.copy, "key")
+        sum_T = sums.tile([P, PACK, P], F32)
+        for t in range(PACK):
+            nc.tensor.transpose(sum_T[:, t, :], position_sum[:, P * t : P * (t + 1)], identity[:])
+        mean_grouped = pool.tile([P, P * PACK], BF16, align_bytes=64)
+        nc.scalar.mul(
+            out=mean_grouped[:].rearrange("p (b t) -> p b t", t=PACK),
+            in_=sum_T[:].rearrange("p t b -> p b t"),
+            mul=1.0 / POSITIONS,
+        )
+        key_codes, key_scales = quantise(nc, pool, key_grouped, D, "key")
+        mean_codes, mean_scales = quantise(nc, pool, mean_grouped, P, "mean")
+
+        erase_grouped = transpose_words(nc, banks, pool, erase_sb, identity, nc.scalar.copy, "erase")
+
+        proj_T = sums.tile([P, PACK, P], F32)
+        for t in range(PACK):
+            rows = slice(P * t, P * (t + 1))
+            one_pass(nc, proj_T[:, t, :], (key_codes[:, rows], key_scales[:, rows]), (mean_codes[:], mean_scales[:]))
+        proj_grouped = pool.tile([P, P * PACK], BF16, align_bytes=64)
+        nc.scalar.copy(
+            out=proj_grouped[:].rearrange("p (b t) -> p b t", t=PACK),
+            in_=proj_T[:].rearrange("p t b -> p b t"),
+        )
+        erase_codes, erase_scales = quantise(nc, pool, erase_grouped, D, "erase")
+        proj_codes, proj_scales = quantise(nc, pool, proj_grouped, P, "proj")
+
+        add_grouped = transpose_words(nc, banks, pool, add_sb, identity, nc.scalar.copy, "add")
+
+        erase_ps = sums.tile([P, D], F32)
+        one_pass(nc, erase_ps[:], (proj_codes[:], proj_scales[:]), (erase_codes[:], erase_scales[:]))
+        keep = pool.tile([P, D], F32)
+        nc.scalar.activation(out=keep[:], in_=erase_ps[:], func=ACT.Sigmoid, scale=-1.0)
+        nc.scalar.activation(out=warm_col[:, 1:2], in_=keep[:, 0:1], func=ACT.Abs_reciprocal_sqrt)
+        add_codes, add_scales = quantise(nc, pool, add_grouped, D, "add")
+        add_ps = sums.tile([P, D], F32)
+        one_pass(nc, add_ps[:], (proj_codes[:], proj_scales[:]), (add_codes[:], add_scales[:]))
+
+        gated = pool.tile([P, SLOTS, D], F32)
+        x = pool.tile([P, SLOTS, D], F32)
+        squares = pool.tile([P, SLOTS, D], F32)
+        normed = pool.tile([P, SLOTS, D], F32)
+        x_sum = pool.tile([P, SLOTS], F32)
+        neg_mean = pool.tile([P, SLOTS], F32)
+        sq_sum = pool.tile([P, SLOTS], F32)
+        rstd = pool.tile([P, SLOTS], F32)
+        shift = pool.tile([P, SLOTS], F32)
+
+        def gate_on_vector(m):
+            cols = slice(0, D if m == 0 else VECTOR_COLUMNS)
+            nc.vector.tensor_tensor(out=gated[:, m, cols], in0=memory_sb[:, m, cols], in1=keep[:, cols], op=ALU.mult)
+
+        def gate_on_gpsimd(m):
+            cols = slice(VECTOR_COLUMNS, D)
+            nc.gpsimd.tensor_tensor(out=gated[:, m, cols], in0=memory_sb[:, m, cols], in1=keep[:, cols], op=ALU.mult)
+
+        def add_and_sum(m):
+            nc.vector.scalar_tensor_tensor(
+                out=x[:, m, :],
+                in0=gated[:, m, :],
+                scalar=1.0,
+                in1=add_ps[:],
+                op0=ALU.mult,
+                op1=ALU.add,
+                accum_out=x_sum[:, m : m + 1],
+            )
+            if m >= SLOTS - VECTOR_NORM_SLOTS:
+                nc.gpsimd.tensor_scalar_mul(out=neg_mean[:, m : m + 1], in0=x_sum[:, m : m + 1], scalar1=-1.0 / D)
+
+        def square_and_sum(m):
+            nc.scalar.activation(
+                out=squares[:, m, :],
+                in_=x[:, m, :],
+                func=ACT.Square,
+                scale=-1.0 * D,
+                bias=x_sum[:, m : m + 1],
+                accum_out=sq_sum[:, m : m + 1],
+            )
+
+        def scale_and_shift(m):
+            nc.scalar.activation(
+                out=rstd[:, m : m + 1],
+                in_=sq_sum[:, m : m + 1],
+                func=ACT.Abs_reciprocal_sqrt,
+                scale=1.0 / (D * D * D),
+                bias=eps_col[:],
+            )
+            if m < SLOTS - VECTOR_NORM_SLOTS:
+                nc.gpsimd.tensor_scalar(
+                    out=shift[:, m : m + 1],
+                    in0=x_sum[:, m : m + 1],
+                    scalar1=rstd[:, m : m + 1],
+                    scalar2=-1.0 / D,
+                    op0=ALU.mult,
+                    op1=ALU.mult,
+                )
+
+        def normalise_and_store(m):
+            col = slice(m, m + 1)
+            if m < SLOTS - VECTOR_NORM_SLOTS:
+                nc.scalar.activation(
+                    out=normed[:, m, :], in_=x[:, m, :], func=ACT.Identity, scale=rstd[:, col], bias=shift[:, col]
+                )
+            else:
+                nc.vector.tensor_scalar(
+                    out=normed[:, m, :],
+                    in0=x[:, m, :],
+                    scalar1=neg_mean[:, col],
+                    scalar2=rstd[:, col],
+                    op0=ALU.add,
+                    op1=ALU.mult,
+                )
+            nc.sync.dma_start(out=out[:, m, :], in_=normed[:, m, :])
+
+        gate_on_vector(0)
+        gate_on_gpsimd(1)
+        for m in range(SLOTS + LAG):
+            if m + 1 < SLOTS:
+                gate_on_vector(m + 1)
+            if m + 2 < SLOTS:
+                gate_on_gpsimd(m + 2)
+            if m < SLOTS:
+                add_and_sum(m)
+                square_and_sum(m)
+            if m >= LAG:
+                normalise_and_store(m - LAG)
+            if m < SLOTS:
+                scale_and_shift(m)

@@ -22,44 +22,48 @@ LN_EPS = 1e-5
 VECTOR_NORM_SLOTS = 4
 GPSIMD_COLUMNS = 256
 VECTOR_COLUMNS = D - GPSIMD_COLUMNS
+WARM_PASSES = 4
 LAG = 2
 
 FLOPS = 3 * 2 * P * D * D
 
 
-def transpose_words(nc, banks, pool, weight_sb, identity, copy_out, name):
+def transpose_half(nc, banks, weight_sb, identity, half, name):
     words = weight_sb[:].bitcast(F32)
-    grouped = pool.tile([P, D * PACK], BF16, align_bytes=64, name=name + "_grouped")
+    bank = banks.tile([P, 2, 2 * P], F32, tag="bank", name=name + "_bank")
+    for u in range(2):
+        for j in range(2):
+            c = 2 * half + j
+            nc.tensor.transpose(
+                bank[:, u, P * j : P * (j + 1)], words[:, WORDS * c + u : WORDS * (c + 1) : 2], identity[:]
+            )
+    return bank
+
+
+def copy_half(copy_out, bank, grouped, half):
     grouped_words = grouped[:].bitcast(F32)
-    for half in range(2):
-        bank = banks.tile([P, 2, 2 * P], F32, tag="bank", name=name + "_bank")
-        for u in range(2):
-            for j in range(2):
-                c = 2 * half + j
-                nc.tensor.transpose(
-                    bank[:, u, P * j : P * (j + 1)], words[:, WORDS * c + u : WORDS * (c + 1) : 2], identity[:]
-                )
-        copy_out(
-            out=grouped_words[:, D * half : D * (half + 1)].rearrange("p (n u) -> p n u", u=2),
-            in_=bank[:].rearrange("p u n -> p n u"),
-        )
-    return grouped
+    copy_out(
+        out=grouped_words[:, D * half : D * (half + 1)].rearrange("p (n u) -> p n u", u=2),
+        in_=bank[:].rearrange("p u n -> p n u"),
+    )
 
 
-def quantise(nc, pool, grouped, columns, name):
-    codes = pool.tile([P, columns], U32, align_bytes=64, name=name + "_codes")
-    scales = pool.tile([P, columns], U8, align_bytes=64, name=name + "_scales")
-    nc.vector.quantize_mx(out=codes[:].bitcast(FP8X4), scales=scales[:], in_=grouped[:])
-    return codes, scales
+def quantise(nc, operand, grouped, columns):
+    codes, scales = operand
+    nc.vector.quantize_mx(
+        out=codes[:, columns].bitcast(FP8X4),
+        scales=scales[:, columns],
+        in_=grouped[:, PACK * columns.start : PACK * columns.stop],
+    )
 
 
-def one_pass(nc, acc, stationary, moving):
+def one_pass(nc, acc, stationary, stationary_columns, moving, moving_columns):
     nc.tensor.matmul_mx(
         out=acc,
-        lhsT=stationary[0].bitcast(FP8X4),
-        lhsT_scale=stationary[1],
-        rhs=moving[0].bitcast(FP8X4),
-        rhs_scale=moving[1],
+        lhsT=stationary[0][:, stationary_columns].bitcast(FP8X4),
+        lhsT_scale=stationary[1][:, stationary_columns],
+        rhs=moving[0][:, moving_columns].bitcast(FP8X4),
+        rhs_scale=moving[1][:, moving_columns],
         start=True,
         stop=True,
     )
@@ -76,7 +80,9 @@ def tile_ultralightweightmemory_pa_s_kernel(
         stack.enter_context(tc.manual_schedule())
 
         iface_sb = pool.tile([P, POSITIONS, D], BF16)
-        nc.sync.dma_start(out=iface_sb[:], in_=interface)
+        for pair in range(2):
+            positions = slice(2 * pair, 2 * pair + 2)
+            nc.sync.dma_start(out=iface_sb[:, positions, :], in_=interface[:, positions, :])
         key_sb = pool.tile([P, CHUNKS * D], BF16)
         key_rows = W_write_key.rearrange("(q c) k -> q (c k)", c=CHUNKS)
         for u in range(2):
@@ -102,53 +108,87 @@ def tile_ultralightweightmemory_pa_s_kernel(
         warm_col = pool.tile([P, 2], F32)
         nc.scalar.activation(out=warm_col[:, 0:1], in_=eps_col[:], func=ACT.Sigmoid)
 
-        pair_sums = pool.tile([P, 2, D], F32)
-        nc.vector.tensor_tensor(out=pair_sums[:], in0=iface_sb[:, 0:2, :], in1=iface_sb[:, 2:4, :], op=ALU.add)
-        position_sum = pool.tile([P, D], F32)
-        nc.vector.tensor_tensor(
-            out=position_sum[:].rearrange("b (t q) -> b t q", t=PACK),
-            in0=pair_sums[:, 0, :].rearrange("b (q t) -> b t q", t=PACK),
-            in1=pair_sums[:, 1, :].rearrange("b (q t) -> b t q", t=PACK),
-            op=ALU.add,
-        )
+        warm_ps = banks.tile([P, WARM_PASSES, P], F32, tag="bank", name="warm_bank")
+        for w in range(WARM_PASSES):
+            nc.tensor.matmul(out=warm_ps[:, w, :], lhsT=identity[:], rhs=identity[:], start=True, stop=True)
 
-        key_grouped = transpose_words(nc, banks, pool, key_sb, identity, nc.scalar.copy, "key")
+        key_grouped = pool.tile([P, D * PACK], BF16, align_bytes=64)
+        erase_grouped = pool.tile([P, D * PACK], BF16, align_bytes=64)
+        add_grouped = pool.tile([P, D * PACK], BF16, align_bytes=64)
+        mean_grouped = pool.tile([P, P * PACK], BF16, align_bytes=64)
+        proj_grouped = pool.tile([P, P * PACK], BF16, align_bytes=64)
+
+        def packed(columns, name):
+            codes = pool.tile([P, columns], U32, align_bytes=64, name=name + "_codes")
+            scales = pool.tile([P, columns], U8, align_bytes=64, name=name + "_scales")
+            return codes, scales
+
+        key_mx = packed(D, "key")
+        erase_mx = packed(D, "erase")
+        add_mx = packed(D, "add")
+        mean_mx = packed(P, "mean")
+        proj_mx = packed(P, "proj")
+        halves = (slice(0, D // 2), slice(D // 2, D))
+        whole = slice(0, P)
+
+        pair_sums = pool.tile([P, 2, D], F32)
+        for pair in range(2):
+            nc.vector.tensor_tensor(
+                out=pair_sums[:, pair, :],
+                in0=iface_sb[:, 2 * pair, :],
+                in1=iface_sb[:, 2 * pair + 1, :],
+                op=ALU.add,
+            )
+        position_sum = pool.tile([P, D], F32)
+        nc.vector.tensor_tensor(out=position_sum[:], in0=pair_sums[:, 0, :], in1=pair_sums[:, 1, :], op=ALU.add)
+
+        key_bank = transpose_half(nc, banks, key_sb, identity, 0, "key")
+        copy_half(nc.scalar.copy, key_bank, key_grouped, 0)
+        key_bank = transpose_half(nc, banks, key_sb, identity, 1, "key")
+        copy_half(nc.vector.tensor_copy, key_bank, key_grouped, 1)
         sum_T = sums.tile([P, PACK, P], F32)
         for t in range(PACK):
-            nc.tensor.transpose(sum_T[:, t, :], position_sum[:, P * t : P * (t + 1)], identity[:])
-        mean_grouped = pool.tile([P, P * PACK], BF16, align_bytes=64)
+            nc.tensor.transpose(sum_T[:, t, :], position_sum[:, t::PACK], identity[:])
         nc.scalar.mul(
             out=mean_grouped[:].rearrange("p (b t) -> p b t", t=PACK),
             in_=sum_T[:].rearrange("p t b -> p b t"),
             mul=1.0 / POSITIONS,
         )
-        key_codes, key_scales = quantise(nc, pool, key_grouped, D, "key")
-        mean_codes, mean_scales = quantise(nc, pool, mean_grouped, P, "mean")
+        quantise(nc, key_mx, key_grouped, halves[0])
+        quantise(nc, key_mx, key_grouped, halves[1])
+        quantise(nc, mean_mx, mean_grouped, whole)
 
-        erase_grouped = transpose_words(nc, banks, pool, erase_sb, identity, nc.scalar.copy, "erase")
+        erase_bank = transpose_half(nc, banks, erase_sb, identity, 0, "erase")
+        copy_half(nc.scalar.copy, erase_bank, erase_grouped, 0)
+        erase_bank = transpose_half(nc, banks, erase_sb, identity, 1, "erase")
+        copy_half(nc.vector.tensor_copy, erase_bank, erase_grouped, 1)
 
         proj_T = sums.tile([P, PACK, P], F32)
         for t in range(PACK):
             rows = slice(P * t, P * (t + 1))
-            one_pass(nc, proj_T[:, t, :], (key_codes[:, rows], key_scales[:, rows]), (mean_codes[:], mean_scales[:]))
-        proj_grouped = pool.tile([P, P * PACK], BF16, align_bytes=64)
+            one_pass(nc, proj_T[:, t, :], key_mx, rows, mean_mx, whole)
         nc.scalar.copy(
             out=proj_grouped[:].rearrange("p (b t) -> p b t", t=PACK),
             in_=proj_T[:].rearrange("p t b -> p b t"),
         )
-        erase_codes, erase_scales = quantise(nc, pool, erase_grouped, D, "erase")
-        proj_codes, proj_scales = quantise(nc, pool, proj_grouped, P, "proj")
+        quantise(nc, erase_mx, erase_grouped, halves[0])
+        quantise(nc, erase_mx, erase_grouped, halves[1])
+        quantise(nc, proj_mx, proj_grouped, whole)
 
-        add_grouped = transpose_words(nc, banks, pool, add_sb, identity, nc.scalar.copy, "add")
+        add_bank = transpose_half(nc, banks, add_sb, identity, 0, "add")
+        copy_half(nc.scalar.copy, add_bank, add_grouped, 0)
+        add_bank = transpose_half(nc, banks, add_sb, identity, 1, "add")
+        copy_half(nc.vector.tensor_copy, add_bank, add_grouped, 1)
 
         erase_ps = sums.tile([P, D], F32)
-        one_pass(nc, erase_ps[:], (proj_codes[:], proj_scales[:]), (erase_codes[:], erase_scales[:]))
+        one_pass(nc, erase_ps[:], proj_mx, whole, erase_mx, slice(0, D))
         keep = pool.tile([P, D], F32)
         nc.scalar.activation(out=keep[:], in_=erase_ps[:], func=ACT.Sigmoid, scale=-1.0)
         nc.scalar.activation(out=warm_col[:, 1:2], in_=keep[:, 0:1], func=ACT.Abs_reciprocal_sqrt)
-        add_codes, add_scales = quantise(nc, pool, add_grouped, D, "add")
+        quantise(nc, add_mx, add_grouped, halves[0])
+        quantise(nc, add_mx, add_grouped, halves[1])
         add_ps = sums.tile([P, D], F32)
-        one_pass(nc, add_ps[:], (proj_codes[:], proj_scales[:]), (add_codes[:], add_scales[:]))
+        one_pass(nc, add_ps[:], proj_mx, whole, add_mx, slice(0, D))
 
         gated = pool.tile([P, SLOTS, D], F32)
         x = pool.tile([P, SLOTS, D], F32)

@@ -19,7 +19,7 @@ PACK = 4
 CHUNKS = D // P
 WORDS = D // 2
 LN_EPS = 1e-5
-VECTOR_NORM_SLOTS = 4
+SCALAR_SLOTS = (0, 1, 2)
 GPSIMD_COLUMNS = 256
 VECTOR_COLUMNS = D - GPSIMD_COLUMNS
 WARM_PASSES = 4
@@ -158,10 +158,13 @@ def tile_ultralightweightmemory_pa_s_kernel(
         quantise(nc, key_mx, key_grouped, halves[1])
         quantise(nc, mean_mx, mean_grouped, whole)
 
-        erase_bank = transpose_half(nc, banks, erase_sb, identity, 0, "erase")
-        copy_half(nc.scalar.copy, erase_bank, erase_grouped, 0)
-        erase_bank = transpose_half(nc, banks, erase_sb, identity, 1, "erase")
-        copy_half(nc.vector.tensor_copy, erase_bank, erase_grouped, 1)
+        for half in range(2):
+            erase_bank = transpose_half(nc, banks, erase_sb, identity, half, "erase")
+            copy_half(nc.scalar.copy, erase_bank, erase_grouped, half)
+        add_bank = transpose_half(nc, banks, add_sb, identity, 0, "add")
+        quantise(nc, erase_mx, erase_grouped, halves[0])
+        copy_half(nc.vector.tensor_copy, add_bank, add_grouped, 0)
+        quantise(nc, erase_mx, erase_grouped, halves[1])
 
         proj_T = sums.tile([P, PACK, P], F32)
         for t in range(PACK):
@@ -171,22 +174,19 @@ def tile_ultralightweightmemory_pa_s_kernel(
             out=proj_grouped[:].rearrange("p (b t) -> p b t", t=PACK),
             in_=proj_T[:].rearrange("p t b -> p b t"),
         )
-        quantise(nc, erase_mx, erase_grouped, halves[0])
-        quantise(nc, erase_mx, erase_grouped, halves[1])
         quantise(nc, proj_mx, proj_grouped, whole)
 
-        add_bank = transpose_half(nc, banks, add_sb, identity, 0, "add")
-        copy_half(nc.scalar.copy, add_bank, add_grouped, 0)
         add_bank = transpose_half(nc, banks, add_sb, identity, 1, "add")
-        copy_half(nc.vector.tensor_copy, add_bank, add_grouped, 1)
+        copy_half(nc.scalar.copy, add_bank, add_grouped, 1)
+        for half in range(2):
+            quantise(nc, add_mx, add_grouped, halves[half])
 
-        erase_ps = sums.tile([P, D], F32)
-        one_pass(nc, erase_ps[:], proj_mx, whole, erase_mx, slice(0, D))
         keep = pool.tile([P, D], F32)
-        nc.scalar.activation(out=keep[:], in_=erase_ps[:], func=ACT.Sigmoid, scale=-1.0)
+        for half in halves:
+            erase_ps = banks.tile([P, D // 2], F32, tag="bank", name="erase_bank")
+            one_pass(nc, erase_ps[:], proj_mx, whole, erase_mx, half)
+            nc.scalar.activation(out=keep[:, half], in_=erase_ps[:], func=ACT.Sigmoid, scale=-1.0)
         nc.scalar.activation(out=warm_col[:, 1:2], in_=keep[:, 0:1], func=ACT.Abs_reciprocal_sqrt)
-        quantise(nc, add_mx, add_grouped, halves[0])
-        quantise(nc, add_mx, add_grouped, halves[1])
         add_ps = sums.tile([P, D], F32)
         one_pass(nc, add_ps[:], proj_mx, whole, add_mx, slice(0, D))
 
@@ -201,14 +201,17 @@ def tile_ultralightweightmemory_pa_s_kernel(
         shift = pool.tile([P, SLOTS], F32)
 
         def gate_on_vector(m):
-            cols = slice(0, D if m == 0 else VECTOR_COLUMNS)
-            nc.vector.tensor_tensor(out=gated[:, m, cols], in0=memory_sb[:, m, cols], in1=keep[:, cols], op=ALU.mult)
+            for cols in halves if m == 0 else (slice(0, VECTOR_COLUMNS),):
+                nc.vector.tensor_tensor(
+                    out=gated[:, m, cols], in0=memory_sb[:, m, cols], in1=keep[:, cols], op=ALU.mult
+                )
 
         def gate_on_gpsimd(m):
             cols = slice(VECTOR_COLUMNS, D)
             nc.gpsimd.tensor_tensor(out=gated[:, m, cols], in0=memory_sb[:, m, cols], in1=keep[:, cols], op=ALU.mult)
 
         def add_and_sum(m):
+            col = slice(m, m + 1)
             nc.vector.scalar_tensor_tensor(
                 out=x[:, m, :],
                 in0=gated[:, m, :],
@@ -216,10 +219,8 @@ def tile_ultralightweightmemory_pa_s_kernel(
                 in1=add_ps[:],
                 op0=ALU.mult,
                 op1=ALU.add,
-                accum_out=x_sum[:, m : m + 1],
+                accum_out=x_sum[:, col],
             )
-            if m >= SLOTS - VECTOR_NORM_SLOTS:
-                nc.gpsimd.tensor_scalar_mul(out=neg_mean[:, m : m + 1], in0=x_sum[:, m : m + 1], scalar1=-1.0 / D)
 
         def square_and_sum(m):
             nc.scalar.activation(
@@ -231,7 +232,10 @@ def tile_ultralightweightmemory_pa_s_kernel(
                 accum_out=sq_sum[:, m : m + 1],
             )
 
-        def scale_and_shift(m):
+        def negated_mean(m):
+            nc.scalar.mul(out=neg_mean[:, m : m + 1], in_=x_sum[:, m : m + 1], mul=-1.0 / D)
+
+        def reciprocal_std(m):
             nc.scalar.activation(
                 out=rstd[:, m : m + 1],
                 in_=sq_sum[:, m : m + 1],
@@ -239,19 +243,20 @@ def tile_ultralightweightmemory_pa_s_kernel(
                 scale=1.0 / (D * D * D),
                 bias=eps_col[:],
             )
-            if m < SLOTS - VECTOR_NORM_SLOTS:
-                nc.gpsimd.tensor_scalar(
-                    out=shift[:, m : m + 1],
-                    in0=x_sum[:, m : m + 1],
-                    scalar1=rstd[:, m : m + 1],
-                    scalar2=-1.0 / D,
-                    op0=ALU.mult,
-                    op1=ALU.mult,
-                )
+
+        def scaled_mean(m):
+            nc.gpsimd.tensor_scalar(
+                out=shift[:, m : m + 1],
+                in0=x_sum[:, m : m + 1],
+                scalar1=rstd[:, m : m + 1],
+                scalar2=-1.0 / D,
+                op0=ALU.mult,
+                op1=ALU.mult,
+            )
 
         def normalise_and_store(m):
             col = slice(m, m + 1)
-            if m < SLOTS - VECTOR_NORM_SLOTS:
+            if m in SCALAR_SLOTS:
                 nc.scalar.activation(
                     out=normed[:, m, :], in_=x[:, m, :], func=ACT.Identity, scale=rstd[:, col], bias=shift[:, col]
                 )
@@ -268,15 +273,19 @@ def tile_ultralightweightmemory_pa_s_kernel(
 
         gate_on_vector(0)
         gate_on_gpsimd(1)
-        for m in range(SLOTS + LAG):
+        for m in range(SLOTS):
             if m + 1 < SLOTS:
                 gate_on_vector(m + 1)
             if m + 2 < SLOTS:
                 gate_on_gpsimd(m + 2)
-            if m < SLOTS:
-                add_and_sum(m)
-                square_and_sum(m)
+            add_and_sum(m)
+            square_and_sum(m)
+            if m not in SCALAR_SLOTS:
+                negated_mean(m)
             if m >= LAG:
                 normalise_and_store(m - LAG)
-            if m < SLOTS:
-                scale_and_shift(m)
+            reciprocal_std(m)
+            if m - 1 in SCALAR_SLOTS:
+                scaled_mean(m - 1)
+        for m in range(SLOTS - LAG, SLOTS):
+            normalise_and_store(m)

@@ -20,6 +20,7 @@ CHUNKS = D // P
 WORDS = D // 2
 LN_EPS = 1e-5
 SCALAR_SLOTS = (0, 1, 2)
+FIRST_SLOTS = 2
 GPSIMD_COLUMNS = 256
 VECTOR_COLUMNS = D - GPSIMD_COLUMNS
 WARM_PASSES = 4
@@ -40,12 +41,18 @@ def transpose_half(nc, banks, weight_sb, identity, half, name):
     return bank
 
 
-def copy_half(copy_out, bank, grouped, half):
-    grouped_words = grouped[:].bitcast(F32)
-    copy_out(
-        out=grouped_words[:, D * half : D * (half + 1)].rearrange("p (n u) -> p n u", u=2),
-        in_=bank[:].rearrange("p u n -> p n u"),
-    )
+def copy_half(copy_out, bank, grouped, half, rows_in_pairs):
+    grouped_words = grouped[:].bitcast(F32)[:, D * half : D * (half + 1)]
+    if rows_in_pairs:
+        copy_out(
+            out=grouped_words.rearrange("p (q j u) -> p q j u", j=2, u=2),
+            in_=bank[:].rearrange("p u (j q) -> p q j u", j=2),
+        )
+    else:
+        copy_out(
+            out=grouped_words.rearrange("p (n u) -> p n u", u=2),
+            in_=bank[:].rearrange("p u n -> p n u"),
+        )
 
 
 def quantise(nc, operand, grouped, columns):
@@ -89,17 +96,15 @@ def tile_ultralightweightmemory_pa_s_kernel(
             half = slice(2 * D * u, 2 * D * (u + 1))
             nc.sync.dma_start(out=key_sb[:, half], in_=key_rows[:, half])
         erase_sb = pool.tile([P, CHUNKS * D], BF16)
-        nc.sync.dma_start(
-            out=erase_sb[:].rearrange("q (c k) -> q c k", c=CHUNKS),
-            in_=W_write_erase.rearrange("(c q) k -> q c k", q=P),
-        )
         add_sb = pool.tile([P, CHUNKS * D], BF16)
-        nc.sync.dma_start(
-            out=add_sb[:].rearrange("q (c k) -> q c k", c=CHUNKS),
-            in_=W_write_add.rearrange("(c q) k -> q c k", q=P),
-        )
+        for weight_sb, weight in ((erase_sb, W_write_erase), (add_sb, W_write_add)):
+            nc.sync.dma_start(
+                out=weight_sb[:].rearrange("q (h e k) -> q h (e k)", h=2, e=2),
+                in_=weight.rearrange("(h q e) k -> q h (e k)", h=2, e=2),
+            )
         memory_sb = pool.tile([P, SLOTS, D], BF16)
-        nc.sync.dma_start(out=memory_sb[:], in_=memory)
+        for slots in (slice(0, FIRST_SLOTS), slice(FIRST_SLOTS, SLOTS)):
+            nc.sync.dma_start(out=memory_sb[:, slots, :], in_=memory[:, slots, :])
 
         identity = pool.tile([P, P], F32)
         make_identity(nc, identity[:])
@@ -143,9 +148,9 @@ def tile_ultralightweightmemory_pa_s_kernel(
         nc.vector.tensor_tensor(out=position_sum[:], in0=pair_sums[:, 0, :], in1=pair_sums[:, 1, :], op=ALU.add)
 
         key_bank = transpose_half(nc, banks, key_sb, identity, 0, "key")
-        copy_half(nc.scalar.copy, key_bank, key_grouped, 0)
+        copy_half(nc.scalar.copy, key_bank, key_grouped, 0, False)
         key_bank = transpose_half(nc, banks, key_sb, identity, 1, "key")
-        copy_half(nc.vector.tensor_copy, key_bank, key_grouped, 1)
+        copy_half(nc.vector.tensor_copy, key_bank, key_grouped, 1, False)
         sum_T = sums.tile([P, PACK, P], F32)
         for t in range(PACK):
             nc.tensor.transpose(sum_T[:, t, :], position_sum[:, t::PACK], identity[:])
@@ -160,11 +165,8 @@ def tile_ultralightweightmemory_pa_s_kernel(
 
         for half in range(2):
             erase_bank = transpose_half(nc, banks, erase_sb, identity, half, "erase")
-            copy_half(nc.scalar.copy, erase_bank, erase_grouped, half)
-        add_bank = transpose_half(nc, banks, add_sb, identity, 0, "add")
-        quantise(nc, erase_mx, erase_grouped, halves[0])
-        copy_half(nc.vector.tensor_copy, add_bank, add_grouped, 0)
-        quantise(nc, erase_mx, erase_grouped, halves[1])
+            copy_half(nc.scalar.copy, erase_bank, erase_grouped, half, True)
+            quantise(nc, erase_mx, erase_grouped, halves[half])
 
         proj_T = sums.tile([P, PACK, P], F32)
         for t in range(PACK):
@@ -176,8 +178,9 @@ def tile_ultralightweightmemory_pa_s_kernel(
         )
         quantise(nc, proj_mx, proj_grouped, whole)
 
-        add_bank = transpose_half(nc, banks, add_sb, identity, 1, "add")
-        copy_half(nc.scalar.copy, add_bank, add_grouped, 1)
+        for half, copy_out in enumerate((nc.scalar.copy, nc.vector.tensor_copy)):
+            add_bank = transpose_half(nc, banks, add_sb, identity, half, "add")
+            copy_half(copy_out, add_bank, add_grouped, half, True)
         for half in range(2):
             quantise(nc, add_mx, add_grouped, halves[half])
 

@@ -21,7 +21,7 @@ WORDS = D // 2
 LN_EPS = 1e-5
 SCALAR_SLOTS = (0, 1, 2)
 FIRST_SLOTS = 2
-GPSIMD_COLUMNS = 256
+GPSIMD_COLUMNS = 320
 VECTOR_COLUMNS = D - GPSIMD_COLUMNS
 WARM_PASSES = 4
 LAG = 2
@@ -248,14 +248,7 @@ def tile_ultralightweightmemory_pa_s_kernel(
             )
 
         def scaled_mean(m):
-            nc.gpsimd.tensor_scalar(
-                out=shift[:, m : m + 1],
-                in0=x_sum[:, m : m + 1],
-                scalar1=rstd[:, m : m + 1],
-                scalar2=-1.0 / D,
-                op0=ALU.mult,
-                op1=ALU.mult,
-            )
+            nc.scalar.mul(out=shift[:, m : m + 1], in_=neg_mean[:, m : m + 1], mul=rstd[:, m : m + 1])
 
         def normalise_and_store(m):
             col = slice(m, m + 1)
@@ -283,12 +276,11 @@ def tile_ultralightweightmemory_pa_s_kernel(
                 gate_on_gpsimd(m + 2)
             add_and_sum(m)
             square_and_sum(m)
-            if m not in SCALAR_SLOTS:
-                negated_mean(m)
+            if m - 1 in SCALAR_SLOTS:
+                scaled_mean(m - 1)
+            negated_mean(m)
             if m >= LAG:
                 normalise_and_store(m - LAG)
             reciprocal_std(m)
-            if m - 1 in SCALAR_SLOTS:
-                scaled_mean(m - 1)
         for m in range(SLOTS - LAG, SLOTS):
             normalise_and_store(m)

@@ -139,9 +139,9 @@ def tile_ultralightweightmemory_pa_s_kernel(
         pair_sums = pool.tile([P, 2, D], F32)
         for pair in range(2):
             nc.vector.tensor_tensor(
-                out=pair_sums[:, pair, :],
-                in0=iface_sb[:, 2 * pair, :],
-                in1=iface_sb[:, 2 * pair + 1, :],
+                out=pair_sums[:, pair, :].rearrange("b (t q) -> b t q", t=PACK),
+                in0=iface_sb[:, 2 * pair, :].rearrange("b (q t) -> b t q", t=PACK),
+                in1=iface_sb[:, 2 * pair + 1, :].rearrange("b (q t) -> b t q", t=PACK),
                 op=ALU.add,
             )
         position_sum = pool.tile([P, D], F32)
@@ -153,7 +153,7 @@ def tile_ultralightweightmemory_pa_s_kernel(
         copy_half(nc.vector.tensor_copy, key_bank, key_grouped, 1, False)
         sum_T = sums.tile([P, PACK, P], F32)
         for t in range(PACK):
-            nc.tensor.transpose(sum_T[:, t, :], position_sum[:, t::PACK], identity[:])
+            nc.tensor.transpose(sum_T[:, t, :], position_sum[:, P * t : P * (t + 1)], identity[:])
         nc.scalar.mul(
             out=mean_grouped[:].rearrange("p (b t) -> p b t", t=PACK),
             in_=sum_T[:].rearrange("p t b -> p b t"),

from contextlib import ExitStack

import concourse.mybir as mybir
from concourse.masks import make_identity

F32 = mybir.dt.float32
BF16 = mybir.dt.bfloat16
U32 = mybir.dt.uint32
U8 = mybir.dt.uint8
FP8X4 = mybir.dt.float8_e4m3fn_x4
ALU = mybir.AluOpType
ACT = mybir.ActivationFunctionType

P = 128
POSITIONS = 4
SLOTS = 8
D = 512
PACK = 4
CHUNKS = D // P
WORDS = D // 2
LN_EPS = 1e-5
SCALAR_SLOTS = (0, 1, 2)
FIRST_SLOTS = 2
GPSIMD_COLUMNS = 320
VECTOR_COLUMNS = D - GPSIMD_COLUMNS
WARM_PASSES = 4
LAG = 2

FLOPS = 3 * 2 * P * D * D


def transpose_half(nc, banks, weight_sb, identity, half, name):
    words = weight_sb[:].bitcast(F32)
    bank = banks.tile([P, 2, 2 * P], F32, tag="bank", name=name + "_bank")
    for u in range(2):
        for j in range(2):
            c = 2 * half + j
            nc.tensor.transpose(
                bank[:, u, P * j : P * (j + 1)], words[:, WORDS * c + u : WORDS * (c + 1) : 2], identity[:]
            )
    return bank


def copy_half(copy_out, bank, grouped, half, rows_in_pairs):
    grouped_words = grouped[:].bitcast(F32)[:, D * half : D * (half + 1)]
    if rows_in_pairs:
        copy_out(
            out=grouped_words.rearrange("p (q j u) -> p q j u", j=2, u=2),
            in_=bank[:].rearrange("p u (j q) -> p q j u", j=2),
        )
    else:
        copy_out(
            out=grouped_words.rearrange("p (n u) -> p n u", u=2),
            in_=bank[:].rearrange("p u n -> p n u"),
        )


def quantise(nc, operand, grouped, columns):
    codes, scales = operand
    nc.vector.quantize_mx(
        out=codes[:, columns].bitcast(FP8X4),
        scales=scales[:, columns],
        in_=grouped[:, PACK * columns.start : PACK * columns.stop],
    )


def one_pass(nc, acc, stationary, stationary_columns, moving, moving_columns):
    nc.tensor.matmul_mx(
        out=acc,
        lhsT=stationary[0][:, stationary_columns].bitcast(FP8X4),
        lhsT_scale=stationary[1][:, stationary_columns],
        rhs=moving[0][:, moving_columns].bitcast(FP8X4),
        rhs_scale=moving[1][:, moving_columns],
        start=True,
        stop=True,
    )


def tile_ultralightweightmemory_pa_s_kernel(
    tc, interface, memory, W_write_key, W_write_erase, W_write_add, out
):
    nc = tc.nc
    with ExitStack() as stack:
        pool = stack.enter_context(tc.tile_pool(name="resident", bufs=1))
        banks = stack.enter_context(tc.psum_pool(name="banks", bufs=4))
        sums = stack.enter_context(tc.psum_pool(name="sums", bufs=1))
        stack.enter_context(tc.manual_schedule())

        iface_sb = pool.tile([P, POSITIONS, D], BF16)
        for pair in range(2):
            positions = slice(2 * pair, 2 * pair + 2)
            nc.sync.dma_start(out=iface_sb[:, positions, :], in_=interface[:, positions, :])
        key_sb = pool.tile([P, CHUNKS * D], BF16)
        key_rows = W_write_key.rearrange("(q c) k -> q (c k)", c=CHUNKS)
        for u in range(2):
            half = slice(2 * D * u, 2 * D * (u + 1))
            nc.sync.dma_start(out=key_sb[:, half], in_=key_rows[:, half])
        erase_sb = pool.tile([P, CHUNKS * D], BF16)
        add_sb = pool.tile([P, CHUNKS * D], BF16)
        for weight_sb, weight in ((erase_sb, W_write_erase), (add_sb, W_write_add)):
            nc.sync.dma_start(
                out=weight_sb[:].rearrange("q (h e k) -> q h (e k)", h=2, e=2),
                in_=weight.rearrange("(h q e) k -> q h (e k)", h=2, e=2),
            )
        memory_sb = pool.tile([P, SLOTS, D], BF16)
        for slots in (slice(0, FIRST_SLOTS), slice(FIRST_SLOTS, SLOTS)):
            nc.sync.dma_start(out=memory_sb[:, slots, :], in_=memory[:, slots, :])

        identity = pool.tile([P, P], F32)
        make_identity(nc, identity[:])
        eps_col = pool.tile([P, 1], F32)
        nc.vector.memset(eps_col[:], LN_EPS)
        warm_col = pool.tile([P, 2], F32)
        nc.scalar.activation(out=warm_col[:, 0:1], in_=eps_col[:], func=ACT.Sigmoid)

        warm_ps = banks.tile([P, WARM_PASSES, P], F32, tag="bank", name="warm_bank")
        for w in range(WARM_PASSES):
            nc.tensor.matmul(out=warm_ps[:, w, :], lhsT=identity[:], rhs=identity[:], start=True, stop=True)

        key_grouped = pool.tile([P, D * PACK], BF16, align_bytes=64)
        erase_grouped = pool.tile([P, D * PACK], BF16, align_bytes=64)
        add_grouped = pool.tile([P, D * PACK], BF16, align_bytes=64)
        mean_grouped = pool.tile([P, P * PACK], BF16, align_bytes=64)
        proj_grouped = pool.tile([P, P * PACK], BF16, align_bytes=64)

        def packed(columns, name):
            codes = pool.tile([P, columns], U32, align_bytes=64, name=name + "_codes")
            scales = pool.tile([P, columns], U8, align_bytes=64, name=name + "_scales")
            return codes, scales

        key_mx = packed(D, "key")
        erase_mx = packed(D, "erase")
        add_mx = packed(D, "add")
        mean_mx = packed(P, "mean")
        proj_mx = packed(P, "proj")
        halves = (slice(0, D // 2), slice(D // 2, D))
        whole = slice(0, P)

        pair_sums = pool.tile([P, 2, D], F32)
        for pair in range(2):
            nc.vector.tensor_tensor(
                out=pair_sums[:, pair, :].rearrange("b (t q) -> b t q", t=PACK),
                in0=iface_sb[:, 2 * pair, :].rearrange("b (q t) -> b t q", t=PACK),
                in1=iface_sb[:, 2 * pair + 1, :].rearrange("b (q t) -> b t q", t=PACK),
                op=ALU.add,
            )
        position_sum = pool.tile([P, D], F32)
        nc.vector.tensor_tensor(out=position_sum[:], in0=pair_sums[:, 0, :], in1=pair_sums[:, 1, :], op=ALU.add)

        key_bank = transpose_half(nc, banks, key_sb, identity, 0, "key")
        copy_half(nc.scalar.copy, key_bank, key_grouped, 0, False)
        key_bank = transpose_half(nc, banks, key_sb, identity, 1, "key")
        copy_half(nc.vector.tensor_copy, key_bank, key_grouped, 1, False)
        sum_T = sums.tile([P, PACK, P], F32)
        for t in range(PACK):
            nc.tensor.transpose(sum_T[:, t, :], position_sum[:, P * t : P * (t + 1)], identity[:])
        nc.scalar.mul(
            out=mean_grouped[:].rearrange("p (b t) -> p b t", t=PACK),
            in_=sum_T[:].rearrange("p t b -> p b t"),
            mul=1.0 / POSITIONS,
        )
        quantise(nc, key_mx, key_grouped, halves[0])
        quantise(nc, key_mx, key_grouped, halves[1])
        quantise(nc, mean_mx, mean_grouped, whole)

        for half in range(2):
            erase_bank = transpose_half(nc, banks, erase_sb, identity, half, "erase")
            copy_half(nc.scalar.copy, erase_bank, erase_grouped, half, True)
            quantise(nc, erase_mx, erase_grouped, halves[half])

        proj_T = sums.tile([P, PACK, P], F32)
        for t in range(PACK):
            rows = slice(P * t, P * (t + 1))
            one_pass(nc, proj_T[:, t, :], key_mx, rows, mean_mx, whole)
        nc.scalar.copy(
            out=proj_grouped[:].rearrange("p (b t) -> p b t", t=PACK),
            in_=proj_T[:].rearrange("p t b -> p b t"),
        )
        quantise(nc, proj_mx, proj_grouped, whole)

        for half, copy_out in enumerate((nc.scalar.copy, nc.vector.tensor_copy)):
            add_bank = transpose_half(nc, banks, add_sb, identity, half, "add")
            copy_half(copy_out, add_bank, add_grouped, half, True)
        for half in range(2):
            quantise(nc, add_mx, add_grouped, halves[half])

        keep = pool.tile([P, D], F32)
        for half in halves:
            erase_ps = banks.tile([P, D // 2], F32, tag="bank", name="erase_bank")
            one_pass(nc, erase_ps[:], proj_mx, whole, erase_mx, half)
            nc.scalar.activation(out=keep[:, half], in_=erase_ps[:], func=ACT.Sigmoid, scale=-1.0)
        nc.scalar.activation(out=warm_col[:, 1:2], in_=keep[:, 0:1], func=ACT.Abs_reciprocal_sqrt)
        add_ps = sums.tile([P, D], F32)
        one_pass(nc, add_ps[:], proj_mx, whole, add_mx, slice(0, D))

        gated = pool.tile([P, SLOTS, D], F32)
        x = pool.tile([P, SLOTS, D], F32)
        squares = pool.tile([P, SLOTS, D], F32)
        normed = pool.tile([P, SLOTS, D], F32)
        x_sum = pool.tile([P, SLOTS], F32)
        neg_mean = pool.tile([P, SLOTS], F32)
        sq_sum = pool.tile([P, SLOTS], F32)
        rstd = pool.tile([P, SLOTS], F32)
        shift = pool.tile([P, SLOTS], F32)

        def gate_on_vector(m):
            for cols in halves if m == 0 else (slice(0, VECTOR_COLUMNS),):
                nc.vector.tensor_tensor(
                    out=gated[:, m, cols], in0=memory_sb[:, m, cols], in1=keep[:, cols], op=ALU.mult
                )

        def gate_on_gpsimd(m):
            cols = slice(VECTOR_COLUMNS, D)
            nc.gpsimd.tensor_tensor(out=gated[:, m, cols], in0=memory_sb[:, m, cols], in1=keep[:, cols], op=ALU.mult)

        def add_and_sum(m):
            col = slice(m, m + 1)
            nc.vector.scalar_tensor_tensor(
                out=x[:, m, :],
                in0=gated[:, m, :],
                scalar=1.0,
                in1=add_ps[:],
                op0=ALU.mult,
                op1=ALU.add,
                accum_out=x_sum[:, col],
            )

        def square_and_sum(m):
            nc.scalar.activation(
                out=squares[:, m, :],
                in_=x[:, m, :],
                func=ACT.Square,
                scale=-1.0 * D,
                bias=x_sum[:, m : m + 1],
                accum_out=sq_sum[:, m : m + 1],
            )

        def negated_mean(m):
            nc.scalar.mul(out=neg_mean[:, m : m + 1], in_=x_sum[:, m : m + 1], mul=-1.0 / D)

        def reciprocal_std(m):
            nc.scalar.activation(
                out=rstd[:, m : m + 1],
                in_=sq_sum[:, m : m + 1],
                func=ACT.Abs_reciprocal_sqrt,
                scale=1.0 / (D * D * D),
                bias=eps_col[:],
            )

        def scaled_mean(m):
            nc.scalar.mul(out=shift[:, m : m + 1], in_=neg_mean[:, m : m + 1], mul=rstd[:, m : m + 1])

        def normalise_and_store(m):
            col = slice(m, m + 1)
            if m in SCALAR_SLOTS:
                nc.scalar.activation(
                    out=normed[:, m, :], in_=x[:, m, :], func=ACT.Identity, scale=rstd[:, col], bias=shift[:, col]
                )
            else:
                nc.vector.tensor_scalar(
                    out=normed[:, m, :],
                    in0=x[:, m, :],
                    scalar1=neg_mean[:, col],
                    scalar2=rstd[:, col],
                    op0=ALU.add,
                    op1=ALU.mult,
                )
            nc.sync.dma_start(out=out[:, m, :], in_=normed[:, m, :])

        gate_on_vector(0)
        gate_on_gpsimd(1)
        for m in range(SLOTS):
            if m + 1 < SLOTS:
                gate_on_vector(m + 1)
            if m + 2 < SLOTS:
                gate_on_gpsimd(m + 2)
            add_and_sum(m)
            square_and_sum(m)
            if m - 1 in SCALAR_SLOTS:
                scaled_mean(m - 1)
            negated_mean(m)
            if m >= LAG:
                normalise_and_store(m - LAG)
            reciprocal_std(m)
        for m in range(SLOTS - LAG, SLOTS):
            normalise_and_store(m)
